import numpy as np
import ml_dtypes

BF16 = ml_dtypes.bfloat16


def bf(x):
    return np.asarray(x, np.float32).astype(BF16)


def f32(x):
    return np.asarray(x, np.float32)


def f64(x):
    return np.asarray(x).astype(np.float64)


def striped(idx):
    return np.tile(idx.reshape(-1, 16).T, (8, 1))


D, V, SM, N = 128, 1024, 128, 1024
LN_EPS = 1e-5


def setup_inputs():
    return {"table": bf(np.random.standard_normal((D, V))), "wq": bf(np.random.standard_normal((D, D)) / np.sqrt(D)), "mem": bf(np.random.standard_normal((SM, D))), "ln_scale": f32(1.0 + 0.1 * np.random.standard_normal((D, 1))), "ln_bias": f32(0.1 * np.random.standard_normal((D, 1))), "offs": striped(np.random.permutation(np.tile(np.arange(V), 2))[:N])}


def reference(table, wq, mem, ln_scale, ln_bias, offs):
    idx = offs[:16].T.reshape(-1)
    q = f64(wq).T @ f64(table)[:, idx]
    sc = f64(mem) @ q / np.sqrt(D)
    e = np.exp(sc - sc.max(axis=0, keepdims=True))
    a = e / e.sum(axis=0, keepdims=True)
    ctx = f64(mem).T @ a
    mu = ctx.mean(axis=0, keepdims=True)
    var = ((ctx - mu) ** 2).mean(axis=0, keepdims=True)
    return (ctx - mu) / np.sqrt(var + LN_EPS) * f64(ln_scale) + f64(ln_bias)

@@ -1,0 +1,147 @@
+import math
+
+import concourse.mybir as mybir
+from concourse.masks import make_identity
+
+BF16 = mybir.dt.bfloat16
+F32 = mybir.dt.float32
+U16 = mybir.dt.uint16
+FUNC = mybir.ActivationFunctionType
+ALU = mybir.AluOpType
+
+P = 128
+V = 1024
+N = 1024
+LN_EPS = 1e-5
+INV_SQRT_D = 1.0 / math.sqrt(P)
+
+PIECE = 512
+PIECES = N // PIECE
+BLOCKS = PIECE // P
+ALL_BLOCKS = N // P
+PSUM_BANKS = 8
+
+FLOPS = 3 * 2 * P * P * N
+
+
+def tile_tmrmodel_kernel(tc, table, wq, mem, ln_scale, ln_bias, offs, out):
+    nc = tc.nc
+    with (
+        tc.tile_pool(name="held", bufs=1) as held,
+        tc.psum_pool(name="psum", bufs=PSUM_BANKS) as psum,
+    ):
+        offsets = held.tile([P, N // 16], U16, name="offsets")
+        nc.sync.dma_start(offsets[:], offs)
+        table_sb = held.tile([P, V], BF16, name="table_sb")
+        nc.sync.dma_start(table_sb[:], table)
+        wq_sb = held.tile([P, P], BF16, name="wq_sb")
+        nc.scalar.dma_start(wq_sb[:], wq)
+        mem_sb = held.tile([P, P], BF16, name="mem_sb")
+        nc.scalar.dma_start(mem_sb[:], mem)
+        gain = held.tile([P, 1], F32, name="gain")
+        nc.sync.dma_start(gain[:], ln_scale)
+        shift = held.tile([P, 1], F32, name="shift")
+        nc.sync.dma_start(shift[:], ln_bias)
+
+        ident_bf = held.tile([P, P], BF16, name="ident_bf")
+        make_identity(nc, ident_bf[:])
+        ident_f32 = held.tile([P, P], F32, name="ident_f32")
+        make_identity(nc, ident_f32[:])
+
+        memT_ps = psum.tile([P, P], BF16, name="memT_ps", tag="bank")
+        nc.tensor.transpose(memT_ps[:], mem_sb[:], ident_bf[:])
+        memT_sb = held.tile([P, P], BF16, name="memT_sb")
+        nc.vector.tensor_copy(memT_sb[:], memT_ps[:])
+
+
+        q_ps = []
+        for i in range(PIECES):
+            q_ps.append(psum.tile([P, PIECE], F32, name=f"q_ps{i}", tag="bank"))
+            piece_offsets = offsets[:, i * (PIECE // 16) : (i + 1) * (PIECE // 16)]
+            nc.tensor.matmul(q_ps[i][:], wq_sb[:], table_sb[:].indirect(piece_offsets), start=True, stop=True)
+
+        q_bf = []
+        for i in range(PIECES):
+            q_bf.append(held.tile([P, PIECE], BF16, name=f"q_bf{i}"))
+            nc.scalar.activation(q_bf[i][:], q_ps[i][:], FUNC.Copy)
+
+        scT_ps = []
+        for i in range(PIECES):
+            scT_ps.append(psum.tile([P, BLOCKS, P], F32, name=f"scT_ps{i}", tag="bank"))
+            for k in range(BLOCKS):
+                nc.tensor.matmul(scT_ps[i][:, k, :], q_bf[i][:, k * P : (k + 1) * P], memT_sb[:], start=True, stop=True)
+
+        exp_bias = []
+        for i in range(PIECES):
+            top = held.tile([P, BLOCKS], F32, name=f"top{i}")
+            nc.vector.reduce_max(top[:], scT_ps[i][:], axis=mybir.AxisListType.X)
+            exp_bias.append(held.tile([P, BLOCKS], F32, name=f"exp_bias{i}"))
+            nc.vector.tensor_scalar(exp_bias[i][:], top[:], -INV_SQRT_D, None, ALU.mult)
+
+        eT = []
+        esum = held.tile([P, ALL_BLOCKS], F32, name="esum")
+        for i in range(PIECES):
+            eT.append(held.tile([P, BLOCKS, P], BF16, name=f"eT{i}"))
+            for k in range(BLOCKS):
+                b = i * BLOCKS + k
+                nc.scalar.activation(
+                    eT[i][:, k, :],
+                    scT_ps[i][:, k, :],
+                    FUNC.Exp,
+                    bias=exp_bias[i][:, k : k + 1],
+                    scale=INV_SQRT_D,
+                    accum_out=esum[:, b : b + 1],
+                )
+
+        e_bf = []
+        for i in range(PIECES):
+            e_ps = psum.tile([P, PIECE], BF16, name=f"e_ps{i}", tag="bank")
+            for k in range(BLOCKS):
+                nc.tensor.transpose(e_ps[:, k * P : (k + 1) * P], eT[i][:, k, :], ident_bf[:])
+            e_bf.append(held.tile([P, PIECE], BF16, name=f"e_bf{i}"))
+            nc.vector.tensor_copy(e_bf[i][:], e_ps[:])
+
+        u_ps = []
+        for i in range(PIECES):
+            u_ps.append(psum.tile([P, BLOCKS, P], F32, name=f"u_ps{i}", tag="bank"))
+            for k in range(BLOCKS):
+                nc.tensor.matmul(u_ps[i][:, k, :], e_bf[i][:, k * P : (k + 1) * P], mem_sb[:], start=True, stop=True)
+
+        stats = held.tile([P, ALL_BLOCKS, 6], F32, name="stats")
+        mean_var = held.tile([P, ALL_BLOCKS, 2], F32, name="mean_var")
+        for i in range(PIECES):
+            for k in range(BLOCKS):
+                b = i * BLOCKS + k
+                nc.vector.bn_stats(stats[:, b, :], u_ps[i][:, k, :])
+                nc.vector.bn_aggr(mean_var[:, b, :], stats[:, b, :])
+
+        sum_sq = held.tile([P, ALL_BLOCKS], F32, name="sum_sq")
+        nc.vector.tensor_tensor(sum_sq[:], esum[:], esum[:], ALU.mult)
+        spread = held.tile([P, ALL_BLOCKS], F32, name="spread")
+        nc.vector.scalar_tensor_tensor(spread[:], sum_sq[:], LN_EPS, mean_var[:, :, 1], ALU.mult, ALU.add)
+        std = held.tile([P, ALL_BLOCKS], F32, name="std")
+        nc.scalar.activation(std[:], spread[:], FUNC.Sqrt)
+        rstd = held.tile([P, ALL_BLOCKS], F32, name="rstd")
+        nc.vector.reciprocal(rstd[:], std[:])
+
+        xhat = []
+        for i in range(PIECES):
+            xhat.append(held.tile([P, BLOCKS, P], F32, name=f"xhat{i}"))
+            for k in range(BLOCKS):
+                b = i * BLOCKS + k
+                nc.vector.tensor_scalar(
+                    xhat[i][:, k, :],
+                    u_ps[i][:, k, :],
+                    mean_var[:, b, 0:1],
+                    rstd[:, b : b + 1],
+                    ALU.subtract,
+                    ALU.mult,
+                )
+
+        for i in range(PIECES):
+            o_ps = psum.tile([P, PIECE], F32, name=f"o_ps{i}", tag="bank")
+            for k in range(BLOCKS):
+                nc.tensor.transpose(o_ps[:, k * P : (k + 1) * P], xhat[i][:, k, :], ident_f32[:])
+            o_sb = held.tile([P, PIECE], F32, name=f"o_sb{i}")
+            nc.scalar.activation(o_sb[:], o_ps[:], FUNC.Identity, bias=shift[:, 0:1], scale=gain[:, 0:1])
+            nc.sync.dma_start(out[:, i * PIECE : (i + 1) * PIECE], o_sb[:])

@@ -19,16 +19,16 @@ PIECE = 512
 PIECES = N // PIECE
 BLOCKS = PIECE // P
 ALL_BLOCKS = N // P
-PSUM_BANKS = 8
 
 FLOPS = 3 * 2 * P * P * N
 
 
 def tile_tmrmodel_kernel(tc, table, wq, mem, ln_scale, ln_bias, offs, out):
     nc = tc.nc
+    blocks = range(ALL_BLOCKS)
     with (
         tc.tile_pool(name="held", bufs=1) as held,
-        tc.psum_pool(name="psum", bufs=PSUM_BANKS) as psum,
+        tc.psum_pool(name="banks", bufs=8) as banks,
     ):
         offsets = held.tile([P, N // 16], U16, name="offsets")
         nc.sync.dma_start(offsets[:], offs)
@@ -36,8 +36,9 @@ def tile_tmrmodel_kernel(tc, table, wq, mem, ln_scale, ln_bias, offs, out):
         nc.sync.dma_start(table_sb[:], table)
         wq_sb = held.tile([P, P], BF16, name="wq_sb")
         nc.scalar.dma_start(wq_sb[:], wq)
-        mem_sb = held.tile([P, P], BF16, name="mem_sb")
-        nc.scalar.dma_start(mem_sb[:], mem)
+        mem_ones = held.tile([P, P + 2], BF16, name="mem_ones")
+        nc.scalar.dma_start(mem_ones[:, 0:P], mem)
+        nc.gpsimd.memset(mem_ones[:, P : P + 2], 1.0)
         gain = held.tile([P, 1], F32, name="gain")
         nc.sync.dma_start(gain[:], ln_scale)
         shift = held.tile([P, 1], F32, name="shift")
@@ -48,100 +49,78 @@ def tile_tmrmodel_kernel(tc, table, wq, mem, ln_scale, ln_bias, offs, out):
         ident_f32 = held.tile([P, P], F32, name="ident_f32")
         make_identity(nc, ident_f32[:])
 
-        memT_ps = psum.tile([P, P], BF16, name="memT_ps", tag="bank")
-        nc.tensor.transpose(memT_ps[:], mem_sb[:], ident_bf[:])
+        memT_ps = banks.tile([P, P], BF16, name="memT_ps", tag="bank")
+        nc.tensor.transpose(memT_ps[:], mem_ones[:, 0:P], ident_bf[:])
         memT_sb = held.tile([P, P], BF16, name="memT_sb")
         nc.vector.tensor_copy(memT_sb[:], memT_ps[:])
 
-
         q_ps = []
         for i in range(PIECES):
-            q_ps.append(psum.tile([P, PIECE], F32, name=f"q_ps{i}", tag="bank"))
+            q_ps.append(banks.tile([P, PIECE], F32, name=f"q_ps{i}", tag="bank"))
             piece_offsets = offsets[:, i * (PIECE // 16) : (i + 1) * (PIECE // 16)]
             nc.tensor.matmul(q_ps[i][:], wq_sb[:], table_sb[:].indirect(piece_offsets), start=True, stop=True)
 
         q_bf = []
-        for i in range(PIECES):
-            q_bf.append(held.tile([P, PIECE], BF16, name=f"q_bf{i}"))
-            nc.scalar.activation(q_bf[i][:], q_ps[i][:], FUNC.Copy)
+        for b in blocks:
+            i, k = divmod(b, BLOCKS)
+            q_bf.append(held.tile([P, P], BF16, name=f"q_bf{b}"))
+            nc.scalar.activation(q_bf[b][:], q_ps[i][:, k * P : (k + 1) * P], FUNC.Copy)
 
         scT_ps = []
-        for i in range(PIECES):
-            scT_ps.append(psum.tile([P, BLOCKS, P], F32, name=f"scT_ps{i}", tag="bank"))
-            for k in range(BLOCKS):
-                nc.tensor.matmul(scT_ps[i][:, k, :], q_bf[i][:, k * P : (k + 1) * P], memT_sb[:], start=True, stop=True)
+        for b in blocks:
+            scT_ps.append(banks.tile([P, P], F32, name=f"scT_ps{b}", tag="bank"))
+            nc.tensor.matmul(scT_ps[b][:], q_bf[b][:], memT_sb[:], start=True, stop=True)
 
         exp_bias = []
-        for i in range(PIECES):
-            top = held.tile([P, BLOCKS], F32, name=f"top{i}")
-            nc.vector.reduce_max(top[:], scT_ps[i][:], axis=mybir.AxisListType.X)
-            exp_bias.append(held.tile([P, BLOCKS], F32, name=f"exp_bias{i}"))
-            nc.vector.tensor_scalar(exp_bias[i][:], top[:], -INV_SQRT_D, None, ALU.mult)
+        for b in blocks:
+            top = held.tile([P, 1], F32, name=f"top{b}")
+            nc.vector.reduce_max(top[:], scT_ps[b][:], axis=mybir.AxisListType.X)
+            exp_bias.append(held.tile([P, 1], F32, name=f"exp_bias{b}"))
+            nc.vector.tensor_scalar(exp_bias[b][:], top[:], -INV_SQRT_D, None, ALU.mult)
 
         eT = []
-        esum = held.tile([P, ALL_BLOCKS], F32, name="esum")
-        for i in range(PIECES):
-            eT.append(held.tile([P, BLOCKS, P], BF16, name=f"eT{i}"))
-            for k in range(BLOCKS):
-                b = i * BLOCKS + k
-                nc.scalar.activation(
-                    eT[i][:, k, :],
-                    scT_ps[i][:, k, :],
-                    FUNC.Exp,
-                    bias=exp_bias[i][:, k : k + 1],
-                    scale=INV_SQRT_D,
-                    accum_out=esum[:, b : b + 1],
-                )
+        for b in blocks:
+            eT.append(held.tile([P, P], BF16, name=f"eT{b}"))
+            nc.scalar.activation(eT[b][:], scT_ps[b][:], FUNC.Exp, bias=exp_bias[b][:], scale=INV_SQRT_D)
 
         e_bf = []
-        for i in range(PIECES):
-            e_ps = psum.tile([P, PIECE], BF16, name=f"e_ps{i}", tag="bank")
-            for k in range(BLOCKS):
-                nc.tensor.transpose(e_ps[:, k * P : (k + 1) * P], eT[i][:, k, :], ident_bf[:])
-            e_bf.append(held.tile([P, PIECE], BF16, name=f"e_bf{i}"))
-            nc.vector.tensor_copy(e_bf[i][:], e_ps[:])
+        for b in blocks:
+            e_ps = banks.tile([P, P], BF16, name=f"e_ps{b}", tag="bank")
+            nc.tensor.transpose(e_ps[:], eT[b][:], ident_bf[:])
+            e_bf.append(held.tile([P, P], BF16, name=f"e_bf{b}"))
+            nc.vector.tensor_copy(e_bf[b][:], e_ps[:])
 
         u_ps = []
-        for i in range(PIECES):
-            u_ps.append(psum.tile([P, BLOCKS, P], F32, name=f"u_ps{i}", tag="bank"))
-            for k in range(BLOCKS):
-                nc.tensor.matmul(u_ps[i][:, k, :], e_bf[i][:, k * P : (k + 1) * P], mem_sb[:], start=True, stop=True)
+        for b in blocks:
+            u_ps.append(banks.tile([P, P + 2], F32, name=f"u_ps{b}", tag="bank"))
+            nc.tensor.matmul(u_ps[b][:], e_bf[b][:], mem_ones[:], start=True, stop=True)
 
-        stats = held.tile([P, ALL_BLOCKS, 6], F32, name="stats")
-        mean_var = held.tile([P, ALL_BLOCKS, 2], F32, name="mean_var")
-        for i in range(PIECES):
-            for k in range(BLOCKS):
-                b = i * BLOCKS + k
-                nc.vector.bn_stats(stats[:, b, :], u_ps[i][:, k, :])
-                nc.vector.bn_aggr(mean_var[:, b, :], stats[:, b, :])
+        mean_var = []
+        eps_s2 = []
+        for b in blocks:
+            stats = held.tile([P, 6], F32, name=f"stats{b}")
+            nc.vector.bn_stats(stats[:], u_ps[b][:, 0:P])
+            mean_var.append(held.tile([P, 2], F32, name=f"mean_var{b}"))
+            nc.vector.bn_aggr(mean_var[b][:], stats[:])
+            eps_s2.append(held.tile([P, 1], F32, name=f"eps_s2{b}"))
+            esum = u_ps[b][:, P : P + 1]
+            nc.vector.tensor_scalar(eps_s2[b][:], esum, esum, LN_EPS, ALU.mult, ALU.mult)
 
-        sum_sq = held.tile([P, ALL_BLOCKS], F32, name="sum_sq")
-        nc.vector.tensor_tensor(sum_sq[:], esum[:], esum[:], ALU.mult)
-        spread = held.tile([P, ALL_BLOCKS], F32, name="spread")
-        nc.vector.scalar_tensor_tensor(spread[:], sum_sq[:], LN_EPS, mean_var[:, :, 1], ALU.mult, ALU.add)
-        std = held.tile([P, ALL_BLOCKS], F32, name="std")
-        nc.scalar.activation(std[:], spread[:], FUNC.Sqrt)
-        rstd = held.tile([P, ALL_BLOCKS], F32, name="rstd")
-        nc.vector.reciprocal(rstd[:], std[:])
+        rstd = []
+        for b in blocks:
+            rstd.append(held.tile([P, 1], F32, name=f"rstd{b}"))
+            nc.scalar.activation(rstd[b][:], mean_var[b][:, 1:2], FUNC.Abs_reciprocal_sqrt, bias=eps_s2[b][:])
 
         xhat = []
-        for i in range(PIECES):
-            xhat.append(held.tile([P, BLOCKS, P], F32, name=f"xhat{i}"))
-            for k in range(BLOCKS):
-                b = i * BLOCKS + k
-                nc.vector.tensor_scalar(
-                    xhat[i][:, k, :],
-                    u_ps[i][:, k, :],
-                    mean_var[:, b, 0:1],
-                    rstd[:, b : b + 1],
-                    ALU.subtract,
-                    ALU.mult,
-                )
+        for b in blocks:
+            xhat.append(held.tile([P, P], F32, name=f"xhat{b}"))
+            nc.vector.tensor_scalar(
+                xhat[b][:], u_ps[b][:, 0:P], mean_var[b][:, 0:1], rstd[b][:], ALU.subtract, ALU.mult
+            )
 
-        for i in range(PIECES):
-            o_ps = psum.tile([P, PIECE], F32, name=f"o_ps{i}", tag="bank")
-            for k in range(BLOCKS):
-                nc.tensor.transpose(o_ps[:, k * P : (k + 1) * P], xhat[i][:, k, :], ident_f32[:])
-            o_sb = held.tile([P, PIECE], F32, name=f"o_sb{i}")
-            nc.scalar.activation(o_sb[:], o_ps[:], FUNC.Identity, bias=shift[:, 0:1], scale=gain[:, 0:1])
-            nc.sync.dma_start(out[:, i * PIECE : (i + 1) * PIECE], o_sb[:])
+        for b in blocks:
+            o_ps = banks.tile([P, P], F32, name=f"o_ps{b}", tag="bank")
+            nc.tensor.transpose(o_ps[:], xhat[b][:], ident_f32[:])
+            o_sb = held.tile([P, P], F32, name=f"o_sb{b}")
+            nc.scalar.activation(o_sb[:], o_ps[:], FUNC.Identity, bias=shift[:], scale=gain[:])
+            nc.sync.dma_start(out[:, b * P : (b + 1) * P], o_sb[:])

@@ -19,8 +19,15 @@ PIECE = 512
 PIECES = N // PIECE
 BLOCKS = PIECE // P
 ALL_BLOCKS = N // P
+IDLE_MATMULS = 4
 
 FLOPS = 3 * 2 * P * P * N
+
+
+def multiply_zeros(nc, banks, zeros, name):
+    idle_ps = banks.tile([P, PIECE], F32, name=name, tag="bank")
+    for r in range(IDLE_MATMULS):
+        nc.tensor.matmul(idle_ps[:], zeros[:, 0:P], zeros[:], start=(r == 0), stop=(r == IDLE_MATMULS - 1))
 
 
 def tile_tmrmodel_kernel(tc, table, wq, mem, ln_scale, ln_bias, offs, out):
@@ -30,6 +37,10 @@ def tile_tmrmodel_kernel(tc, table, wq, mem, ln_scale, ln_bias, offs, out):
         tc.tile_pool(name="held", bufs=1) as held,
         tc.psum_pool(name="banks", bufs=8) as banks,
     ):
+        zeros = held.tile([P, PIECE], BF16, name="zeros")
+        nc.gpsimd.memset(zeros[:], 0.0)
+        multiply_zeros(nc, banks, zeros, "idle_ps_loads")
+
         offsets = held.tile([P, N // 16], U16, name="offsets")
         nc.sync.dma_start(offsets[:], offs)
         table_sb = held.tile([P, V], BF16, name="table_sb")
@@ -92,8 +103,12 @@ def tile_tmrmodel_kernel(tc, table, wq, mem, ln_scale, ln_bias, offs, out):
 
         u_ps = []
         for b in blocks:
-            u_ps.append(banks.tile([P, P + 2], F32, name=f"u_ps{b}", tag="bank"))
-            nc.tensor.matmul(u_ps[b][:], e_bf[b][:], mem_ones[:], start=True, stop=True)
+            if b % 2 == 0:
+                u_pair = banks.tile([P, 2, P + 2], F32, name=f"u_pair{b}", tag="bank")
+            u_ps.append(u_pair[:, b % 2, :])
+            nc.tensor.matmul(u_ps[b], e_bf[b][:], mem_ones[:], start=True, stop=True)
+
+        multiply_zeros(nc, banks, zeros, "idle_ps_norm")
 
         mean_var = []
         eps_s2 = []

@@ -75,7 +75,7 @@ def tile_tmrmodel_kernel(tc, table, wq, mem, ln_scale, ln_bias, offs, out):
         for b in blocks:
             i, k = divmod(b, BLOCKS)
             q_bf.append(held.tile([P, P], BF16, name=f"q_bf{b}"))
-            nc.scalar.activation(q_bf[b][:], q_ps[i][:, k * P : (k + 1) * P], FUNC.Copy)
+            nc.scalar.activation(q_bf[b][:], q_ps[i][:, k * P : (k + 1) * P], FUNC.Copy, scale=INV_SQRT_D)
 
         scT_ps = []
         for b in blocks:
@@ -84,15 +84,13 @@ def tile_tmrmodel_kernel(tc, table, wq, mem, ln_scale, ln_bias, offs, out):
 
         exp_bias = []
         for b in blocks:
-            top = held.tile([P, 1], F32, name=f"top{b}")
-            nc.vector.reduce_max(top[:], scT_ps[b][:], axis=mybir.AxisListType.X)
             exp_bias.append(held.tile([P, 1], F32, name=f"exp_bias{b}"))
-            nc.vector.tensor_scalar(exp_bias[b][:], top[:], -INV_SQRT_D, None, ALU.mult)
+            nc.vector.reduce_max(exp_bias[b][:], scT_ps[b][:], axis=mybir.AxisListType.X, negate=True)
 
         eT = []
         for b in blocks:
             eT.append(held.tile([P, P], BF16, name=f"eT{b}"))
-            nc.scalar.activation(eT[b][:], scT_ps[b][:], FUNC.Exp, bias=exp_bias[b][:], scale=INV_SQRT_D)
+            nc.scalar.activation(eT[b][:], scT_ps[b][:], FUNC.Exp, bias=exp_bias[b][:])
 
         e_bf = []
         for b in blocks:

@@ -15,19 +15,21 @@ N = 1024
 LN_EPS = 1e-5
 INV_SQRT_D = 1.0 / math.sqrt(P)
 
-PIECE = 512
+BANK = 512
+PIECE = 256
 PIECES = N // PIECE
 BLOCKS = PIECE // P
 ALL_BLOCKS = N // P
-IDLE_MATMULS = 4
+IDLE_MATMULS_LOADS = 3
+IDLE_MATMULS_NORM = 4
 
 FLOPS = 3 * 2 * P * P * N
 
 
-def multiply_zeros(nc, banks, zeros, name):
-    idle_ps = banks.tile([P, PIECE], F32, name=name, tag="bank")
-    for r in range(IDLE_MATMULS):
-        nc.tensor.matmul(idle_ps[:], zeros[:, 0:P], zeros[:], start=(r == 0), stop=(r == IDLE_MATMULS - 1))
+def multiply_zeros(nc, banks, zeros, name, count):
+    idle_ps = banks.tile([P, BANK], F32, name=name, tag="bank")
+    for r in range(count):
+        nc.tensor.matmul(idle_ps[:], zeros[:, 0:P], zeros[:], start=(r == 0), stop=(r == count - 1))
 
 
 def tile_tmrmodel_kernel(tc, table, wq, mem, ln_scale, ln_bias, offs, out):
@@ -37,16 +39,16 @@ def tile_tmrmodel_kernel(tc, table, wq, mem, ln_scale, ln_bias, offs, out):
         tc.tile_pool(name="held", bufs=1) as held,
         tc.psum_pool(name="banks", bufs=8) as banks,
     ):
-        zeros = held.tile([P, PIECE], BF16, name="zeros")
+        zeros = held.tile([P, BANK], BF16, name="zeros")
         nc.gpsimd.memset(zeros[:], 0.0)
-        multiply_zeros(nc, banks, zeros, "idle_ps_loads")
+        multiply_zeros(nc, banks, zeros, "idle_ps_loads", IDLE_MATMULS_LOADS)
 
-        offsets = held.tile([P, N // 16], U16, name="offsets")
-        nc.sync.dma_start(offsets[:], offs)
         table_sb = held.tile([P, V], BF16, name="table_sb")
         nc.sync.dma_start(table_sb[:], table)
+        offsets = held.tile([P, N // 16], U16, name="offsets")
+        nc.sync.dma_start(offsets[:], offs)
         wq_sb = held.tile([P, P], BF16, name="wq_sb")
-        nc.scalar.dma_start(wq_sb[:], wq)
+        nc.sync.dma_start(wq_sb[:], wq)
         mem_ones = held.tile([P, P + 2], BF16, name="mem_ones")
         nc.scalar.dma_start(mem_ones[:, 0:P], mem)
         nc.gpsimd.memset(mem_ones[:, P : P + 2], 1.0)
@@ -75,7 +77,10 @@ def tile_tmrmodel_kernel(tc, table, wq, mem, ln_scale, ln_bias, offs, out):
         for b in blocks:
             i, k = divmod(b, BLOCKS)
             q_bf.append(held.tile([P, P], BF16, name=f"q_bf{b}"))
-            nc.scalar.activation(q_bf[b][:], q_ps[i][:, k * P : (k + 1) * P], FUNC.Copy, scale=INV_SQRT_D)
+            if b < ALL_BLOCKS // 2:
+                nc.vector.tensor_scalar(q_bf[b][:], q_ps[i][:, k * P : (k + 1) * P], INV_SQRT_D, None, ALU.mult)
+            else:
+                nc.scalar.activation(q_bf[b][:], q_ps[i][:, k * P : (k + 1) * P], FUNC.Copy, scale=INV_SQRT_D)
 
         scT_ps = []
         for b in blocks:
@@ -106,7 +111,7 @@ def tile_tmrmodel_kernel(tc, table, wq, mem, ln_scale, ln_bias, offs, out):
             u_ps.append(u_pair[:, b % 2, :])
             nc.tensor.matmul(u_ps[b], e_bf[b][:], mem_ones[:], start=True, stop=True)
 
-        multiply_zeros(nc, banks, zeros, "idle_ps_norm")
+        multiply_zeros(nc, banks, zeros, "idle_ps_norm", IDLE_MATMULS_NORM)
 
         mean_var = []
         eps_s2 = []

@@ -74,18 +74,18 @@ def tile_tmrmodel_kernel(tc, table, wq, mem, ln_scale, ln_bias, offs, out):
             nc.tensor.matmul(q_ps[i][:], wq_sb[:], table_sb[:].indirect(piece_offsets), start=True, stop=True)
 
         q_bf = []
-        for b in blocks:
-            i, k = divmod(b, BLOCKS)
-            q_bf.append(held.tile([P, P], BF16, name=f"q_bf{b}"))
-            if b < ALL_BLOCKS // 2:
-                nc.vector.tensor_scalar(q_bf[b][:], q_ps[i][:, k * P : (k + 1) * P], INV_SQRT_D, None, ALU.mult)
+        for i in range(PIECES):
+            q_bf.append(held.tile([P, PIECE], BF16, name=f"q_bf{i}"))
+            if i < PIECES // 2:
+                nc.vector.tensor_scalar(q_bf[i][:], q_ps[i][:], INV_SQRT_D, None, ALU.mult)
             else:
-                nc.scalar.activation(q_bf[b][:], q_ps[i][:, k * P : (k + 1) * P], FUNC.Copy, scale=INV_SQRT_D)
+                nc.scalar.activation(q_bf[i][:], q_ps[i][:], FUNC.Copy, scale=INV_SQRT_D)
 
         scT_ps = []
         for b in blocks:
+            i, k = divmod(b, BLOCKS)
             scT_ps.append(banks.tile([P, P], F32, name=f"scT_ps{b}", tag="bank"))
-            nc.tensor.matmul(scT_ps[b][:], q_bf[b][:], memT_sb[:], start=True, stop=True)
+            nc.tensor.matmul(scT_ps[b][:], q_bf[i][:, k * P : (k + 1) * P], memT_sb[:], start=True, stop=True)
 
         exp_bias = []
         for b in blocks:
@@ -99,17 +99,21 @@ def tile_tmrmodel_kernel(tc, table, wq, mem, ln_scale, ln_bias, offs, out):
 
         e_bf = []
         for b in blocks:
-            e_ps = banks.tile([P, P], BF16, name=f"e_ps{b}", tag="bank")
-            nc.tensor.transpose(e_ps[:], eT[b][:], ident_bf[:])
-            e_bf.append(held.tile([P, P], BF16, name=f"e_bf{b}"))
-            nc.vector.tensor_copy(e_bf[b][:], e_ps[:])
+            if b % 2 == 0:
+                e_ps = banks.tile([P, 2 * P], BF16, name=f"e_ps{b}", tag="bank")
+                e_pair = held.tile([P, 2 * P], BF16, name=f"e_pair{b}")
+            half = slice((b % 2) * P, (b % 2 + 1) * P)
+            nc.tensor.transpose(e_ps[:, half], eT[b][:], ident_bf[:])
+            e_bf.append(e_pair[:, half])
+            if b % 2 == 1:
+                nc.vector.tensor_copy(e_pair[:], e_ps[:])
 
         u_ps = []
         for b in blocks:
             if b % 2 == 0:
                 u_pair = banks.tile([P, 2, P + 2], F32, name=f"u_pair{b}", tag="bank")
             u_ps.append(u_pair[:, b % 2, :])
-            nc.tensor.matmul(u_ps[b], e_bf[b][:], mem_ones[:], start=True, stop=True)
+            nc.tensor.matmul(u_ps[b], e_bf[b], mem_ones[:], start=True, stop=True)
 
         multiply_zeros(nc, banks, zeros, "idle_ps_norm", IDLE_MATMULS_NORM)
 
@@ -137,8 +141,10 @@ def tile_tmrmodel_kernel(tc, table, wq, mem, ln_scale, ln_bias, offs, out):
             )
 
         for b in blocks:
-            o_ps = banks.tile([P, P], F32, name=f"o_ps{b}", tag="bank")
-            nc.tensor.transpose(o_ps[:], xhat[b][:], ident_f32[:])
-            o_sb = held.tile([P, P], F32, name=f"o_sb{b}")
-            nc.scalar.activation(o_sb[:], o_ps[:], FUNC.Identity, bias=shift[:], scale=gain[:])
-            nc.sync.dma_start(out[:, b * P : (b + 1) * P], o_sb[:])
+            if b % 2 == 0:
+                o_ps = banks.tile([P, 2 * P], F32, name=f"o_ps{b}", tag="bank")
+            nc.tensor.transpose(o_ps[:, (b % 2) * P : (b % 2 + 1) * P], xhat[b][:], ident_f32[:])
+            if b % 2 == 1:
+                o_sb = held.tile([P, 2 * P], F32, name=f"o_sb{b}")
+                nc.scalar.activation(o_sb[:], o_ps[:], FUNC.Identity, bias=shift[:], scale=gain[:])
+                nc.sync.dma_start(out[:, (b - 1) * P : (b + 1) * P], o_sb[:])

@@ -44,14 +44,14 @@ def tile_tmrmodel_kernel(tc, table, wq, mem, ln_scale, ln_bias, offs, out):
         multiply_zeros(nc, banks, zeros, "idle_ps_loads", IDLE_MATMULS_LOADS)
 
         table_sb = held.tile([P, V], BF16, name="table_sb")
-        nc.sync.dma_start(table_sb[:], table)
+        nc.scalar.dma_start(table_sb[:], table)
+        mem_ones = held.tile([P, P + 2], BF16, name="mem_ones")
+        nc.sync.dma_start(mem_ones[:, 0:P], mem)
+        nc.gpsimd.memset(mem_ones[:, P : P + 2], 1.0)
         offsets = held.tile([P, N // 16], U16, name="offsets")
         nc.sync.dma_start(offsets[:], offs)
         wq_sb = held.tile([P, P], BF16, name="wq_sb")
         nc.sync.dma_start(wq_sb[:], wq)
-        mem_ones = held.tile([P, P + 2], BF16, name="mem_ones")
-        nc.scalar.dma_start(mem_ones[:, 0:P], mem)
-        nc.gpsimd.memset(mem_ones[:, P : P + 2], 1.0)
         gain = held.tile([P, 1], F32, name="gain")
         nc.sync.dma_start(gain[:], ln_scale)
         shift = held.tile([P, 1], F32, name="shift")

@@ -52,15 +52,16 @@ def tile_tmrmodel_kernel(tc, table, wq, mem, ln_scale, ln_bias, offs, out):
         nc.sync.dma_start(offsets[:], offs)
         wq_sb = held.tile([P, P], BF16, name="wq_sb")
         nc.sync.dma_start(wq_sb[:], wq)
-        gain = held.tile([P, 1], F32, name="gain")
-        nc.sync.dma_start(gain[:], ln_scale)
-        shift = held.tile([P, 1], F32, name="shift")
-        nc.sync.dma_start(shift[:], ln_bias)
 
         ident_bf = held.tile([P, P], BF16, name="ident_bf")
         make_identity(nc, ident_bf[:])
         ident_f32 = held.tile([P, P], F32, name="ident_f32")
         make_identity(nc, ident_f32[:])
+
+        gain = held.tile([P, 1], F32, name="gain")
+        nc.gpsimd.dma_start(gain[:], ln_scale)
+        shift = held.tile([P, 1], F32, name="shift")
+        nc.gpsimd.dma_start(shift[:], ln_bias)
 
         memT_ps = banks.tile([P, P], BF16, name="memT_ps", tag="bank")
         nc.tensor.transpose(memT_ps[:], mem_ones[:, 0:P], ident_bf[:])

import math

import concourse.mybir as mybir
from concourse.masks import make_identity

BF16 = mybir.dt.bfloat16
F32 = mybir.dt.float32
U16 = mybir.dt.uint16
FUNC = mybir.ActivationFunctionType
ALU = mybir.AluOpType

P = 128
V = 1024
N = 1024
LN_EPS = 1e-5
INV_SQRT_D = 1.0 / math.sqrt(P)

BANK = 512
PIECE = 256
PIECES = N // PIECE
BLOCKS = PIECE // P
ALL_BLOCKS = N // P
IDLE_MATMULS_LOADS = 3
IDLE_MATMULS_NORM = 4

FLOPS = 3 * 2 * P * P * N


def multiply_zeros(nc, banks, zeros, name, count):
    idle_ps = banks.tile([P, BANK], F32, name=name, tag="bank")
    for r in range(count):
        nc.tensor.matmul(idle_ps[:], zeros[:, 0:P], zeros[:], start=(r == 0), stop=(r == count - 1))


def tile_tmrmodel_kernel(tc, table, wq, mem, ln_scale, ln_bias, offs, out):
    nc = tc.nc
    blocks = range(ALL_BLOCKS)
    with (
        tc.tile_pool(name="held", bufs=1) as held,
        tc.psum_pool(name="banks", bufs=8) as banks,
    ):
        zeros = held.tile([P, BANK], BF16, name="zeros")
        nc.gpsimd.memset(zeros[:], 0.0)
        multiply_zeros(nc, banks, zeros, "idle_ps_loads", IDLE_MATMULS_LOADS)

        table_sb = held.tile([P, V], BF16, name="table_sb")
        nc.scalar.dma_start(table_sb[:], table)
        mem_ones = held.tile([P, P + 2], BF16, name="mem_ones")
        nc.sync.dma_start(mem_ones[:, 0:P], mem)
        nc.gpsimd.memset(mem_ones[:, P : P + 2], 1.0)
        offsets = held.tile([P, N // 16], U16, name="offsets")
        nc.sync.dma_start(offsets[:], offs)
        wq_sb = held.tile([P, P], BF16, name="wq_sb")
        nc.sync.dma_start(wq_sb[:], wq)

        ident_bf = held.tile([P, P], BF16, name="ident_bf")
        make_identity(nc, ident_bf[:])
        ident_f32 = held.tile([P, P], F32, name="ident_f32")
        make_identity(nc, ident_f32[:])

        gain = held.tile([P, 1], F32, name="gain")
        nc.gpsimd.dma_start(gain[:], ln_scale)
        shift = held.tile([P, 1], F32, name="shift")
        nc.gpsimd.dma_start(shift[:], ln_bias)

        memT_ps = banks.tile([P, P], BF16, name="memT_ps", tag="bank")
        nc.tensor.transpose(memT_ps[:], mem_ones[:, 0:P], ident_bf[:])
        memT_sb = held.tile([P, P], BF16, name="memT_sb")
        nc.vector.tensor_copy(memT_sb[:], memT_ps[:])

        q_ps = []
        for i in range(PIECES):
            q_ps.append(banks.tile([P, PIECE], F32, name=f"q_ps{i}", tag="bank"))
            piece_offsets = offsets[:, i * (PIECE // 16) : (i + 1) * (PIECE // 16)]
            nc.tensor.matmul(q_ps[i][:], wq_sb[:], table_sb[:].indirect(piece_offsets), start=True, stop=True)

        q_bf = []
        for i in range(PIECES):
            q_bf.append(held.tile([P, PIECE], BF16, name=f"q_bf{i}"))
            if i < PIECES // 2:
                nc.vector.tensor_scalar(q_bf[i][:], q_ps[i][:], INV_SQRT_D, None, ALU.mult)
            else:
                nc.scalar.activation(q_bf[i][:], q_ps[i][:], FUNC.Copy, scale=INV_SQRT_D)

        scT_ps = []
        for b in blocks:
            i, k = divmod(b, BLOCKS)
            scT_ps.append(banks.tile([P, P], F32, name=f"scT_ps{b}", tag="bank"))
            nc.tensor.matmul(scT_ps[b][:], q_bf[i][:, k * P : (k + 1) * P], memT_sb[:], start=True, stop=True)

        exp_bias = []
        for b in blocks:
            exp_bias.append(held.tile([P, 1], F32, name=f"exp_bias{b}"))
            nc.vector.reduce_max(exp_bias[b][:], scT_ps[b][:], axis=mybir.AxisListType.X, negate=True)

        eT = []
        for b in blocks:
            eT.append(held.tile([P, P], BF16, name=f"eT{b}"))
            nc.scalar.activation(eT[b][:], scT_ps[b][:], FUNC.Exp, bias=exp_bias[b][:])

        e_bf = []
        for b in blocks:
            if b % 2 == 0:
                e_ps = banks.tile([P, 2 * P], BF16, name=f"e_ps{b}", tag="bank")
                e_pair = held.tile([P, 2 * P], BF16, name=f"e_pair{b}")
            half = slice((b % 2) * P, (b % 2 + 1) * P)
            nc.tensor.transpose(e_ps[:, half], eT[b][:], ident_bf[:])
            e_bf.append(e_pair[:, half])
            if b % 2 == 1:
                nc.vector.tensor_copy(e_pair[:], e_ps[:])

        u_ps = []
        for b in blocks:
            if b % 2 == 0:
                u_pair = banks.tile([P, 2, P + 2], F32, name=f"u_pair{b}", tag="bank")
            u_ps.append(u_pair[:, b % 2, :])
            nc.tensor.matmul(u_ps[b], e_bf[b], mem_ones[:], start=True, stop=True)

        multiply_zeros(nc, banks, zeros, "idle_ps_norm", IDLE_MATMULS_NORM)

        mean_var = []
        eps_s2 = []
        for b in blocks:
            stats = held.tile([P, 6], F32, name=f"stats{b}")
            nc.vector.bn_stats(stats[:], u_ps[b][:, 0:P])
            mean_var.append(held.tile([P, 2], F32, name=f"mean_var{b}"))
            nc.vector.bn_aggr(mean_var[b][:], stats[:])
            eps_s2.append(held.tile([P, 1], F32, name=f"eps_s2{b}"))
            esum = u_ps[b][:, P : P + 1]
            nc.vector.tensor_scalar(eps_s2[b][:], esum, esum, LN_EPS, ALU.mult, ALU.mult)

        rstd = []
        for b in blocks:
            rstd.append(held.tile([P, 1], F32, name=f"rstd{b}"))
            nc.scalar.activation(rstd[b][:], mean_var[b][:, 1:2], FUNC.Abs_reciprocal_sqrt, bias=eps_s2[b][:])

        xhat = []
        for b in blocks:
            xhat.append(held.tile([P, P], F32, name=f"xhat{b}"))
            nc.vector.tensor_scalar(
                xhat[b][:], u_ps[b][:, 0:P], mean_var[b][:, 0:1], rstd[b][:], ALU.subtract, ALU.mult
            )

        for b in blocks:
            if b % 2 == 0:
                o_ps = banks.tile([P, 2 * P], F32, name=f"o_ps{b}", tag="bank")
            nc.tensor.transpose(o_ps[:, (b % 2) * P : (b % 2 + 1) * P], xhat[b][:], ident_f32[:])
            if b % 2 == 1:
                o_sb = held.tile([P, 2 * P], F32, name=f"o_sb{b}")
                nc.scalar.activation(o_sb[:], o_ps[:], FUNC.Identity, bias=shift[:], scale=gain[:])
                nc.sync.dma_start(out[:, (b - 1) * P : (b + 1) * P], o_sb[:])
